import numpy as np
import ml_dtypes


def mxq(x, axis, fmt="e4m3"):
    dtype, down = {"e4m3": (ml_dtypes.float8_e4m3fn, 7), "e5m2": (ml_dtypes.float8_e5m2, 14)}[fmt]
    v = np.moveaxis(np.asarray(x, np.float32).astype(ml_dtypes.bfloat16).astype(np.float64), axis, -1)
    blocks = v.reshape(v.shape[:-1] + (-1, 32))
    amax = np.abs(blocks).max(-1, keepdims=True)
    byte = np.maximum(np.where(amax > 0, np.frexp(amax)[1] - 1 + 127, 0) - down, 1)
    scale = np.exp2(byte - 127.0)
    codes = (blocks / scale).astype(np.float32).astype(dtype).astype(np.float64)
    return np.moveaxis((codes * scale).reshape(v.shape), -1, axis)


WIDE = False


def mx_kscale(k):
    if not WIDE:
        return np.ones(k)
    levels = np.array([10, -10, 5, -5, 0])
    if k % 512:
        return np.exp2(np.random.permutation(np.resize(levels, k // 32))).repeat(32)
    a = np.empty((k // 512, 16))
    for p in range(k // 512):
        a[p, :8] = np.random.permutation(np.resize(levels, 8))
        for g in range(8):
            far = levels[np.abs(levels - a[p, g]) >= 10]
            a[p, g + 8] = far[np.random.randint(len(far))]
    return np.exp2(a.ravel()).repeat(32)


BF16 = ml_dtypes.bfloat16


def bf(x):
    return np.asarray(x, np.float32).astype(BF16)


def f64(x):
    return np.asarray(x).astype(np.float64)


E2M1 = np.array([0.0, 0.5, 1.0, 1.5, 2.0, 3.0, 4.0, 6.0, -0.0, -0.5, -1.0, -1.5, -2.0, -3.0, -4.0, -6.0])


def pack_weight(w, fmt):
    k, n = w.shape
    w = f64(bf(w)).reshape(k // 32, 32, n)
    amax = np.abs(w).max(1)
    if fmt == "e4m3":
        byte = np.frexp(amax)[1] - 1 + 127 - 7
    else:
        mant, ex = np.frexp(amax / 6.0)
        byte = np.where(mant > 0.5, ex, ex - 1) + 127
    byte = np.clip(np.where(amax > 0, byte, 1), 1, 254)
    scaled = (w * np.exp2(127.0 - byte)[:, None, :]).reshape(k, n).astype(np.float32)
    by_word = np.ascontiguousarray(scaled.reshape(k // 512, 128, 4, n).transpose(0, 1, 3, 2))
    if fmt == "e4m3":
        words = by_word.astype(ml_dtypes.float8_e4m3fn).view(np.uint8)
    else:
        c = by_word.astype(ml_dtypes.float4_e2m1fn).view(np.uint8) & 0xF
        words = c[..., 0::2] | (c[..., 1::2] << 4)
    return np.ascontiguousarray(words), np.ascontiguousarray(byte.astype(np.uint8).reshape(k // 512, 16, n))


def unpack_weight(words, scales, fmt):
    g, p, n, _ = words.shape
    if fmt == "e4m3":
        vals = np.ascontiguousarray(words).view(ml_dtypes.float8_e4m3fn).astype(np.float64)
    else:
        nib = np.empty((g, p, n, 4), np.uint8)
        nib[..., 0::2] = words & 0xF
        nib[..., 1::2] = words >> 4
        vals = E2M1[nib]
    vals = vals * np.repeat(np.exp2(scales.astype(np.float64) - 127.0), 8, axis=1)[..., None]
    return vals.transpose(0, 1, 3, 2).reshape(g * 512, n)


B, T, C, R, H, DN, DR, DV = 2, 256, 2048, 512, 16, 128, 64, 128
DQ = DN + DR
NF = DR // 2


def rotate_half(u):
    u1, u2 = u[..., : u.shape[-1] // 2], u[..., u.shape[-1] // 2 :]
    return np.concatenate([-u2, u1], axis=-1)


def draw0():
    s, t = mx_kscale(C), mx_kscale(R)
    x = bf(np.random.standard_normal((B, T, C)) * s)
    freqs_cis = bf(np.stack([np.random.uniform(size=(T, NF)), np.random.uniform(size=(T, NF))], axis=-1))
    w_kv_down_words, w_kv_down_scales = pack_weight(np.random.standard_normal((C, R)) / np.sqrt(C) / s[:, None] * t, "e4m3")
    w_k_up_words, w_k_up_scales = pack_weight(np.random.standard_normal((R, H * DQ)) / np.sqrt(R) / t[:, None], "e4m3")
    w_v_up_words, w_v_up_scales = pack_weight(np.random.standard_normal((R, H * DV)) / np.sqrt(R) / t[:, None], "e4m3")
    return {
        "x": x,
        "freqs_cis": freqs_cis,
        "w_kv_down_words": w_kv_down_words,
        "w_kv_down_scales": w_kv_down_scales,
        "w_k_up_words": w_k_up_words,
        "w_k_up_scales": w_k_up_scales,
        "w_v_up_words": w_v_up_words,
        "w_v_up_scales": w_v_up_scales,
    }


def core(x, freqs_cis, w_kv_down_words, w_kv_down_scales, w_k_up_words, w_k_up_scales, w_v_up_words, w_v_up_scales):
    kv = mxq(f64(x), 2, "e4m3") @ unpack_weight(w_kv_down_words, w_kv_down_scales, "e4m3")
    kvq = mxq(kv, 2, "e4m3")
    k = (kvq @ unpack_weight(w_k_up_words, w_k_up_scales, "e4m3")).reshape(B, T, H, DQ)
    v = (kvq @ unpack_weight(w_v_up_words, w_v_up_scales, "e4m3")).reshape(B, T, H, DV)
    k_nope, k_rope = k[..., :DN], k[..., DN:]
    freqs = f64(freqs_cis)
    cos = freqs[..., 0][None, :, None, :]
    sin = freqs[..., 1][None, :, None, :]
    rep = DR // cos.shape[-1]
    cos = np.tile(cos, (1, 1, 1, rep))
    sin = np.tile(sin, (1, 1, 1, rep))
    k_rope = k_rope * cos + rotate_half(k_rope) * sin
    return np.concatenate([k_nope, k_rope], axis=-1), v


def e4m3fn_bytes(y):
    return np.clip(np.asarray(y, np.float64), -448.0, 448.0).astype(np.float32).astype(ml_dtypes.float8_e4m3fn).view(np.uint8)


def e4m3fn_values(b):
    return np.asarray(b, np.uint8).view(ml_dtypes.float8_e4m3fn).astype(np.float64)


def setup_inputs():
    d = draw0()
    x0 = np.asarray(d['x']).astype(np.float64)
    s = (np.max(np.abs(x0), axis=(0, 1), keepdims=True) / 448.0).astype(np.float32)
    out = {}
    for k, v in d.items():
        if k == 'x':
            out['x_bytes'] = e4m3fn_bytes(x0 / s.astype(np.float64))
            out['x_scale'] = s
        else:
            out[k] = v
    return out


def reference(x_bytes, x_scale, freqs_cis, w_kv_down_words, w_kv_down_scales, w_k_up_words, w_k_up_scales, w_v_up_words, w_v_up_scales):
    return core(e4m3fn_values(x_bytes) * x_scale.astype(np.float64), freqs_cis, w_kv_down_words, w_kv_down_scales, w_k_up_words, w_k_up_scales, w_v_up_words, w_v_up_scales)

@@ -1,0 +1,467 @@
+from contextlib import ExitStack
+
+import concourse.mybir as mybir
+from concourse.masks import make_identity
+
+F32 = mybir.dt.float32
+BF16 = mybir.dt.bfloat16
+I32 = mybir.dt.int32
+U8 = mybir.dt.uint8
+E4M3 = mybir.dt.float8_e4m3fn
+E4M3X4 = mybir.dt.float8_e4m3fn_x4
+MULT = mybir.AluOpType.mult
+ADD = mybir.AluOpType.add
+
+B, T, C, R, H, DN, DR, DV = 2, 256, 2048, 512, 16, 128, 64, 128
+DQ = DN + DR
+P = 128
+K_PASS = 512
+G = C // K_PASS
+TILES = B * T // P
+FLOPS = 2 * B * T * (C * R + R * H * (DQ + DV))
+
+
+def tile_fa3mlaattention_pa_w8_kernel(
+    tc,
+    x_bytes,
+    x_scale,
+    freqs_cis,
+    w_kv_down_words,
+    w_kv_down_scales,
+    w_k_up_words,
+    w_k_up_scales,
+    w_v_up_words,
+    w_v_up_scales,
+    out_k,
+    out_v,
+):
+    nc = tc.nc
+    x_rows = x_bytes.rearrange("b (p j) k -> b p j k", p=P)
+    k_rows = out_k.rearrange("b (p j) h d -> b p j h d", p=P)
+    v_rows = out_v.rearrange("b (p j) h d -> b p j (h d)", p=P)
+
+    with ExitStack() as ctx:
+        keep = ctx.enter_context(tc.tile_pool(name="keep", bufs=1))
+        tok = ctx.enter_context(tc.tile_pool(name="tok", bufs=TILES))
+        rot = ctx.enter_context(tc.tile_pool(name="rot", bufs=8))
+        psum = ctx.enter_context(tc.psum_pool(name="psum", bufs=8))
+        ctx.enter_context(tc.manual_schedule())
+
+        def bank():
+            b = psum.tile([P, 512], F32, name="bank", tag="bank")
+            return b
+
+        sd = keep.tile([P, R], U8, align_bytes=64)
+        sv = keep.tile([P, 512], U8, align_bytes=64)
+        sk = keep.tile([P, 768], U8, align_bytes=64)
+        for plane in (sd, sv, sk):
+            nc.vector.memset(plane[:].bitcast(I32), 0)
+
+        wd = keep.tile([P, G, R], I32, align_bytes=64)
+        wv = keep.tile([P, H * DV], I32, align_bytes=64)
+        wk = keep.tile([P, H * DQ], I32, align_bytes=64)
+
+        x_pair = []
+        for b in range(B):
+            x_u8 = keep.tile([P, 2, C], U8, align_bytes=64, name="x_u8_%d" % b)
+            x_pair.append(x_u8)
+        xu = [x_pair[i // 2][:, i % 2, :] for i in range(TILES)]
+
+        def load_x(i, a, b):
+            nc.sync.dma_start(out=xu[i][:, a:b], in_=x_rows[i // 2][:, i % 2, a:b])
+
+        def load_scales(plane, rows_of_quadrant):
+            for q in range(4):
+                nc.sync.dma_start(out=plane[32 * q : 32 * q + 16, :].bitcast(I32), in_=rows_of_quadrant(q).bitcast(I32))
+
+        load_x(0, 0, C // 2)
+        load_x(0, C // 2, C)
+        load_x(1, 0, C)
+        load_scales(sd, lambda q: w_kv_down_scales[:, 4 * q : 4 * q + 4, :])
+        for g in (0, 2):
+            nc.sync.dma_start(
+                out=wd[:, g : g + 2, :],
+                in_=w_kv_down_words[g : g + 2].rearrange("g p n t -> p g (n t)").bitcast(I32),
+            )
+        load_scales(sv, lambda q: w_v_up_scales[0, 4 * q : 4 * q + 4, :].rearrange("r (c n) -> c r n", c=4))
+        nc.sync.dma_start(out=wv[:], in_=w_v_up_words[0].rearrange("p n t -> p (n t)").bitcast(I32))
+        nc.sync.dma_start(out=x_pair[1][:], in_=x_rows[1])
+        load_scales(sk, lambda q: w_k_up_scales[0, 4 * q : 4 * q + 4, :].rearrange("r (c n) -> c r n", c=4))
+        nc.sync.dma_start(out=wk[:], in_=w_k_up_words[0].rearrange("p n t -> p (n t)").bitcast(I32))
+        xs = keep.tile([P, G, 4], F32)
+        nc.gpsimd.dma_start(out=xs[:], in_=x_scale.rearrange("o q (g p t) -> p (o q g) t", p=P, t=4))
+        cs = keep.tile([P, 2, DR], BF16)
+        nc.gpsimd.dma_start(out=cs[:], in_=freqs_cis.rearrange("(p c) j e -> p c (j e)", p=P))
+        ident = keep.tile([P, P], F32)
+        make_identity(nc, ident[:])
+
+        cos = keep.tile([P, 2, 2, 32], F32)
+        sin = keep.tile([P, 2, 2, 32], F32)
+
+        def make_tables():
+            nc.gpsimd.tensor_copy(out=cos[:, :, 0, :], in_=cs[:, :, 0::2])
+            nc.gpsimd.tensor_copy(out=cos[:, :, 1, :], in_=cs[:, :, 0::2])
+            nc.gpsimd.tensor_scalar(out=sin[:, :, 0, :], in0=cs[:, :, 1::2], scalar1=-1.0, scalar2=None, op0=MULT)
+            nc.gpsimd.tensor_copy(out=sin[:, :, 1, :], in_=cs[:, :, 1::2])
+
+        make_tables()
+
+        xb, xq, xqs, acc, kvw, kvq, kvs, ko, vo = ({} for n in range(9))
+
+        def cast(i, a, b, engine="s"):
+            if i not in xb:
+                x_bf = tok.tile([P, C], BF16, align_bytes=64)
+                xb[i] = x_bf
+            src = xu[i][:, 512 * a : 512 * b].bitcast(E4M3)
+            if engine == "v":
+                nc.vector.tensor_copy(out=xb[i][:, 512 * a : 512 * b], in_=src)
+            else:
+                nc.scalar.copy(out=xb[i][:, 512 * a : 512 * b], in_=src)
+
+        xt = {}
+
+        def turn_x(i, half):
+            words = xb[i][:].bitcast(F32)
+            t = bank()
+            xt[i, half] = t
+            for j in range(4):
+                g, u = 2 * half + j // 2, j % 2
+                nc.tensor.transpose(t[:, P * j : P * (j + 1)], words[:, 256 * g + u : 256 * (g + 1) : 2], ident[:])
+
+        def scale_x(i):
+            x_g = tok.tile([P, G, P * 4], BF16, align_bytes=64)
+            x_c = tok.tile([P, G * P], I32, align_bytes=64)
+            x_s = tok.tile([P, G * P], U8, align_bytes=64)
+            xq[i], xqs[i] = x_c, x_s
+
+            def product(g):
+                view = xt[i, g // 2][:].bitcast(BF16)[:, 512 * (g % 2) : 512 * (g % 2 + 1)]
+                nc.vector.tensor_tensor(
+                    out=x_g[:, g, :].rearrange("p (r u e) -> p r u e", u=2, e=2),
+                    in0=view.rearrange("p (u r e) -> p r u e", u=2, e=2),
+                    in1=xs[:, g, :].unsqueeze(1).to_broadcast([P, P, 4]).rearrange("p r (u e) -> p r u e", e=2),
+                    op=MULT,
+                )
+
+            def quantise(half):
+                nc.vector.quantize_mx(
+                    out=x_c[:, 256 * half : 256 * (half + 1)].bitcast(E4M3X4),
+                    scales=x_s[:, 256 * half : 256 * (half + 1)],
+                    in_=x_g[:, 2 * half : 2 * half + 2, :].rearrange("p g n -> p (g n)"),
+                )
+
+            x_ops[i] = (product, quantise)
+
+        x_ops = {}
+
+        def product_x(i, g):
+            if i not in x_ops:
+                scale_x(i)
+            x_ops[i][0](g)
+
+        def quantise_x(i, half):
+            x_ops[i][1](half)
+
+        def down(i, half):
+            if half == 0:
+                a = bank()
+                acc[i] = a
+            a = acc[i]
+            for g in (2 * half, 2 * half + 1):
+                nc.tensor.matmul_mx(
+                    a[:],
+                    lhsT=xq[i][:, P * g : P * (g + 1)].bitcast(E4M3X4),
+                    lhsT_scale=xqs[i][:, P * g : P * (g + 1)],
+                    rhs=wd[:, g, :].bitcast(E4M3X4),
+                    rhs_scale=sd[4 * g : P, :],
+                    start=(g == 0),
+                    stop=(g == G - 1),
+                )
+
+        def round_kv(i, a=0, b=2, engine="s"):
+            if i not in kvw:
+                kv_b = tok.tile([P, R], BF16, align_bytes=64)
+                kvw[i] = kv_b
+            copy_out(engine, kvw[i][:, 256 * a : 256 * b], acc[i][:, 256 * a : 256 * b])
+
+        def turn_kv(i):
+            t = bank()
+            xt[i, "kv"] = t
+            words = kvw[i][:].bitcast(F32)
+            for u in range(2):
+                nc.tensor.transpose(t[:, P * u : P * (u + 1)], words[:, u::2], ident[:])
+
+        def gather_kv(i, engine="v"):
+            kv_g = tok.tile([P, R], BF16, align_bytes=64)
+            kvw[i] = kv_g
+            copy_out(
+                engine,
+                kv_g[:].bitcast(F32).rearrange("p (r u) -> p r u", u=2),
+                xt[i, "kv"][:, 0:256].rearrange("p (u r) -> p r u", u=2),
+            )
+
+        def quantise_kv(i):
+            kv_c = tok.tile([P, P], I32, align_bytes=64)
+            kv_s = tok.tile([P, P], U8, align_bytes=64)
+            kvq[i], kvs[i] = kv_c, kv_s
+            nc.vector.quantize_mx(out=kv_c[:].bitcast(E4M3X4), scales=kv_s[:], in_=kvw[i][:])
+
+        def up(i, out, codes, scales):
+            nc.tensor.matmul_mx(
+                out,
+                lhsT=kvq[i][:].bitcast(E4M3X4),
+                lhsT_scale=kvs[i][:],
+                rhs=codes.bitcast(E4M3X4),
+                rhs_scale=scales,
+                start=True,
+                stop=True,
+            )
+
+        def copy_out(engine, out, in_):
+            if engine == "v":
+                nc.vector.tensor_copy(out=out, in_=in_)
+            else:
+                nc.scalar.copy(out=out, in_=in_)
+
+        banks = {}
+
+        def begin_out(i):
+            k_sb = tok.tile([P, H, DQ], F32, align_bytes=64)
+            v_sb = tok.tile([P, H * DV], F32, align_bytes=64)
+            ko[i], vo[i] = k_sb, v_sb
+
+        def mm_v(i, c):
+            b = bank()
+            banks["v", i, c] = b
+            up(i, b[:], wv[:, 512 * c : 512 * (c + 1)], sv[4 * c : P, :])
+
+        def ev_v(i, c, engine="s"):
+            copy_out(engine, vo[i][:, 512 * c : 512 * (c + 1)], banks["v", i, c][:])
+
+        def store_v(i, c0, c1):
+            nc.sync.dma_start(out=v_rows[i // 2][:, i % 2, 512 * c0 : 512 * c1], in_=vo[i][:, 512 * c0 : 512 * c1])
+
+        def mm_n(i, c):
+            b = bank()
+            banks["n", i, c] = b
+            for j in range(4):
+                h = 4 * c + j
+                up(i, b[:, DN * j : DN * (j + 1)], wk[:, DQ * h : DQ * h + DN], sk[4 * c : P, DQ * j : DQ * j + DN])
+
+        def ev_n(i, c, engine="s"):
+            copy_out(engine, ko[i][:, 4 * c : 4 * c + 4, 0:DN], banks["n", i, c][:].rearrange("p (h d) -> p h d", d=DN))
+
+        wr = keep.tile([P, H, DR], I32, align_bytes=64)
+        sr = keep.tile([P, 4, DR], U8, align_bytes=64)
+
+        def gather_rope_weights(half):
+            heads = wk[:].rearrange("p (h d) -> p h d", d=DQ)[:, 8 * half : 8 * half + 8, DN:DQ]
+            nc.vector.tensor_copy(out=wr[:, 8 * half : 8 * half + 8, :], in_=heads)
+
+        def gather_rope_scales():
+            nc.vector.tensor_copy(
+                out=sr[:].bitcast(I32), in_=sk[:].bitcast(I32).rearrange("p (h d) -> p h d", d=DQ // 4)[:, :, DN // 4 : DQ // 4]
+            )
+
+        def mm_r(i, half):
+            b = bank()
+            banks["r", i, half] = b
+            for j in range(2):
+                c = 2 * half + j
+                up(
+                    i,
+                    b[:, 256 * j : 256 * (j + 1)],
+                    wr[:, 4 * c : 4 * c + 4, :].rearrange("p h d -> p (h d)"),
+                    sr[4 * c : P].rearrange("p h d -> p (h d)"),
+                )
+
+        def ev_r(i, half, add_engine="g"):
+            r = banks["r", i, half][:].rearrange("p (h a j) -> p h a j", a=2, j=32)
+            rc = rot.tile([P, 8, 2, 32], F32)
+            rs = rot.tile([P, 8, 2, 32], F32)
+            par = i % 2
+            cb = cos[:, par].unsqueeze(1).to_broadcast([P, 8, 2, 32])
+            sb = sin[:, par].unsqueeze(1).to_broadcast([P, 8, 2, 32])
+            nc.vector.tensor_tensor(out=rc[:], in0=r, in1=cb, op=MULT)
+            nc.vector.tensor_tensor(out=rs[:], in0=r[:, :, ::-1, :], in1=sb, op=MULT)
+            eng = nc.gpsimd if add_engine == "g" else nc.vector
+            eng.tensor_tensor(
+                out=ko[i][:, 8 * half : 8 * half + 8, DN:DQ],
+                in0=rc[:].rearrange("p h a j -> p h (a j)"),
+                in1=rs[:].rearrange("p h a j -> p h (a j)"),
+                op=ADD,
+            )
+
+        def store_k(i, h0, h1):
+            hs = slice(8 * h0, 8 * h1)
+            nc.sync.dma_start(out=k_rows[i // 2][:, i % 2, hs, :], in_=ko[i][:, hs, :])
+
+        cast(0, 0, 1, "v")
+        cast(0, 1, 2)
+        turn_x(0, 0)
+        cast(0, 3, 4)
+        cast(0, 2, 3, "v")
+        product_x(0, 0)
+        product_x(0, 1)
+        turn_x(0, 1)
+        cast(1, 0, 2)
+        product_x(0, 2)
+        quantise_x(0, 0)
+        turn_x(1, 0)
+        product_x(0, 3)
+        down(0, 0)
+        quantise_x(0, 1)
+        cast(1, 2, 4)
+        down(0, 1)
+        product_x(1, 1)
+        turn_x(1, 1)
+        product_x(1, 0)
+        product_x(1, 2)
+        quantise_x(1, 0)
+        round_kv(0, 1, 2)
+        round_kv(0, 0, 1)
+        turn_kv(0)
+        down(1, 0)
+        gather_kv(0, "s")
+        product_x(1, 3)
+        quantise_kv(0)
+        quantise_x(1, 1)
+        mm_v(0, 0)
+        down(1, 1)
+        cast(3, 0, 2, "v")
+        begin_out(0)
+        ev_v(0, 0)
+        store_v(0, 0, 1)
+        mm_v(0, 1)
+        turn_x(3, 0)
+        round_kv(1, 0, 2)
+        cast(2, 0, 2, "v")
+        turn_kv(1)
+        mm_v(0, 2)
+        cast(3, 2, 4, "v")
+        ev_v(0, 1)
+        store_v(0, 1, 2)
+        gather_rope_scales()
+        mm_v(0, 3)
+        product_x(3, 0)
+        gather_kv(1, "s")
+        turn_x(3, 1)
+        quantise_kv(1)
+        product_x(3, 1)
+        product_x(3, 2)
+        ev_v(0, 2)
+        ev_v(0, 3)
+        store_v(0, 2, 4)
+        mm_v(1, 0)
+        mm_v(1, 1)
+        mm_v(1, 3)
+        begin_out(1)
+        ev_v(1, 0)
+        gather_rope_weights(1)
+        ev_v(1, 1)
+        store_v(1, 0, 2)
+        ev_v(1, 3)
+        mm_r(1, 1)
+        product_x(3, 3)
+        mm_n(1, 3)
+        mm_v(1, 2)
+        ev_v(1, 2)
+        store_v(1, 2, 4)
+        mm_r(0, 1)
+        mm_n(1, 2)
+        mm_n(1, 0)
+        mm_n(0, 3)
+        ev_n(1, 2)
+        ev_n(1, 3)
+        ev_r(1, 1)
+        store_k(1, 1, 2)
+        gather_rope_weights(0)
+        mm_n(0, 0)
+        ev_r(0, 1)
+        quantise_x(3, 0)
+        mm_r(0, 0)
+        mm_n(0, 2)
+        mm_n(0, 1)
+        quantise_x(3, 1)
+        ev_n(0, 3)
+        mm_r(1, 0)
+        down(3, 0)
+        ev_n(0, 2)
+        store_k(0, 1, 2)
+        ev_r(0, 0)
+        down(3, 1)
+        ev_n(0, 1)
+        mm_n(1, 1)
+        turn_x(2, 0)
+        ev_n(0, 0)
+        store_k(0, 0, 1)
+        ev_r(1, 0)
+        round_kv(3, 0, 2)
+        cast(2, 2, 4)
+        product_x(2, 0)
+        turn_kv(3)
+        gather_kv(3, "s")
+        ev_n(1, 0)
+        quantise_kv(3)
+        turn_x(2, 1)
+        mm_v(3, 0)
+        mm_r(3, 0)
+        mm_v(3, 1)
+        ev_n(1, 1)
+        store_k(1, 0, 1)
+        product_x(2, 1)
+        mm_v(3, 3)
+        product_x(2, 2)
+        product_x(2, 3)
+        mm_v(3, 2)
+        quantise_x(2, 0)
+        begin_out(3)
+        ev_v(3, 0)
+        ev_v(3, 1)
+        store_v(3, 0, 2)
+        quantise_x(2, 1)
+        mm_r(3, 1)
+        mm_n(3, 1)
+        ev_v(3, 2)
+        down(2, 0)
+        ev_v(3, 3)
+        store_v(3, 2, 4)
+        ev_n(3, 1)
+        down(2, 1)
+        mm_n(3, 0)
+        round_kv(2, 0, 2)
+        mm_n(3, 2)
+        turn_kv(2)
+        mm_n(3, 3)
+        ev_r(3, 0)
+        ev_r(3, 1)
+        ev_n(3, 0)
+        store_k(3, 0, 1)
+        gather_kv(2)
+        quantise_kv(2)
+        ev_n(3, 2, "v")
+        mm_v(2, 1)
+        mm_r(2, 0)
+        begin_out(2)
+        ev_r(2, 0)
+        mm_v(2, 2)
+        ev_n(3, 3)
+        store_k(3, 1, 2)
+        ev_v(2, 1)
+        mm_v(2, 3)
+        mm_v(2, 0)
+        mm_n(2, 0)
+        ev_v(2, 0, "v")
+        ev_v(2, 2)
+        mm_r(2, 1)
+        mm_n(2, 2)
+        mm_n(2, 3)
+        ev_v(2, 3)
+        store_v(2, 0, 4)
+        mm_n(2, 1)
+        ev_n(2, 0)
+        ev_n(2, 2)
+        ev_n(2, 3)
+        ev_n(2, 1)
+        ev_r(2, 1, "v")
+        store_k(2, 0, 2)

@@ -53,10 +53,15 @@ def tile_fa3mlaattention_pa_w8_kernel(
 
         sd = keep.tile([P, R], U8, align_bytes=64)
         sv = keep.tile([P, 512], U8, align_bytes=64)
-        sk = keep.tile([P, 768], U8, align_bytes=64)
-        for plane in (sd, sv, sk):
+        sk = keep.tile([P, H * DQ], U8, align_bytes=64)
+        xs_rows = keep.tile([P, K_PASS], F32)
+        nc.vector.memset(xs_rows[:], 0.0)
+        for plane in (sd, sv):
             nc.vector.memset(plane[:].bitcast(I32), 0)
 
+        ident = keep.tile([P, P], F32)
+        make_identity(nc, ident[:])
+        nc.gpsimd.memset(sk[:].bitcast(I32), 0)
         wd = keep.tile([P, G, R], I32, align_bytes=64)
         wv = keep.tile([P, H * DV], I32, align_bytes=64)
         wk = keep.tile([P, H * DQ], I32, align_bytes=64)
@@ -65,35 +70,33 @@ def tile_fa3mlaattention_pa_w8_kernel(
         for b in range(B):
             x_u8 = keep.tile([P, 2, C], U8, align_bytes=64, name="x_u8_%d" % b)
             x_pair.append(x_u8)
+        xs = keep.tile([P, G, 4], F32)
         xu = [x_pair[i // 2][:, i % 2, :] for i in range(TILES)]
 
         def load_x(i, a, b):
             nc.sync.dma_start(out=xu[i][:, a:b], in_=x_rows[i // 2][:, i % 2, a:b])
 
-        def load_scales(plane, rows_of_quadrant):
+        def load_scales(plane, rows_of_quadrant, parts=16):
             for q in range(4):
-                nc.sync.dma_start(out=plane[32 * q : 32 * q + 16, :].bitcast(I32), in_=rows_of_quadrant(q).bitcast(I32))
+                nc.sync.dma_start(out=plane[32 * q : 32 * q + parts, :].bitcast(I32), in_=rows_of_quadrant(q).bitcast(I32))
 
-        load_x(0, 0, C // 2)
-        load_x(0, C // 2, C)
-        load_x(1, 0, C)
+        load_x(0, 0, C)
+        nc.sync.dma_start(out=xs_rows[0:G, :], in_=x_scale.rearrange("o q (g k) -> (o q g) k", g=G))
         load_scales(sd, lambda q: w_kv_down_scales[:, 4 * q : 4 * q + 4, :])
+        load_x(1, 0, C)
         for g in (0, 2):
             nc.sync.dma_start(
                 out=wd[:, g : g + 2, :],
                 in_=w_kv_down_words[g : g + 2].rearrange("g p n t -> p g (n t)").bitcast(I32),
             )
-        load_scales(sv, lambda q: w_v_up_scales[0, 4 * q : 4 * q + 4, :].rearrange("r (c n) -> c r n", c=4))
+        load_x(2, 0, C)
         nc.sync.dma_start(out=wv[:], in_=w_v_up_words[0].rearrange("p n t -> p (n t)").bitcast(I32))
-        nc.sync.dma_start(out=x_pair[1][:], in_=x_rows[1])
-        load_scales(sk, lambda q: w_k_up_scales[0, 4 * q : 4 * q + 4, :].rearrange("r (c n) -> c r n", c=4))
+        load_scales(sv, lambda q: w_v_up_scales[0, 4 * q : 4 * q + 4, :].rearrange("r (c n) -> c r n", c=4))
         nc.sync.dma_start(out=wk[:], in_=w_k_up_words[0].rearrange("p n t -> p (n t)").bitcast(I32))
-        xs = keep.tile([P, G, 4], F32)
-        nc.gpsimd.dma_start(out=xs[:], in_=x_scale.rearrange("o q (g p t) -> p (o q g) t", p=P, t=4))
+        load_scales(sk, lambda q: w_k_up_scales[0, 4 * q : 4 * q + 4, :], parts=4)
+        load_x(3, 0, C)
         cs = keep.tile([P, 2, DR], BF16)
         nc.gpsimd.dma_start(out=cs[:], in_=freqs_cis.rearrange("(p c) j e -> p c (j e)", p=P))
-        ident = keep.tile([P, P], F32)
-        make_identity(nc, ident[:])
 
         cos = keep.tile([P, 2, 2, 32], F32)
         sin = keep.tile([P, 2, 2, 32], F32)
@@ -105,6 +108,17 @@ def tile_fa3mlaattention_pa_w8_kernel(
             nc.gpsimd.tensor_copy(out=sin[:, :, 1, :], in_=cs[:, :, 1::2])
 
         make_tables()
+
+        xs_bank = []
+
+        def turn_scale():
+            t = bank()
+            xs_bank.append(t)
+            for j in range(4):
+                nc.tensor.transpose(t[:, P * j : P * (j + 1)], xs_rows[:, j::4], ident[:])
+
+        def copy_scale():
+            nc.vector.tensor_copy(out=xs[:], in_=xs_bank[0][:].rearrange("p (t r) -> p r t", t=4)[:, 0:G, :])
 
         xb, xq, xqs, acc, kvw, kvq, kvs, ko, vo = ({} for n in range(9))
 
@@ -246,36 +260,24 @@ def tile_fa3mlaattention_pa_w8_kernel(
             banks["n", i, c] = b
             for j in range(4):
                 h = 4 * c + j
-                up(i, b[:, DN * j : DN * (j + 1)], wk[:, DQ * h : DQ * h + DN], sk[4 * c : P, DQ * j : DQ * j + DN])
+                up(i, b[:, DN * j : DN * (j + 1)], wk[:, DQ * h : DQ * h + DN], sk[:, DQ * h : DQ * h + DN])
 
         def ev_n(i, c, engine="s"):
             copy_out(engine, ko[i][:, 4 * c : 4 * c + 4, 0:DN], banks["n", i, c][:].rearrange("p (h d) -> p h d", d=DN))
 
-        wr = keep.tile([P, H, DR], I32, align_bytes=64)
-        sr = keep.tile([P, 4, DR], U8, align_bytes=64)
-
-        def gather_rope_weights(half):
-            heads = wk[:].rearrange("p (h d) -> p h d", d=DQ)[:, 8 * half : 8 * half + 8, DN:DQ]
-            nc.vector.tensor_copy(out=wr[:, 8 * half : 8 * half + 8, :], in_=heads)
-
-        def gather_rope_scales():
-            nc.vector.tensor_copy(
-                out=sr[:].bitcast(I32), in_=sk[:].bitcast(I32).rearrange("p (h d) -> p h d", d=DQ // 4)[:, :, DN // 4 : DQ // 4]
-            )
-
         def mm_r(i, half):
             b = bank()
             banks["r", i, half] = b
-            for j in range(2):
-                c = 2 * half + j
+            for j in range(8):
+                h = 8 * half + j
                 up(
                     i,
-                    b[:, 256 * j : 256 * (j + 1)],
-                    wr[:, 4 * c : 4 * c + 4, :].rearrange("p h d -> p (h d)"),
-                    sr[4 * c : P].rearrange("p h d -> p (h d)"),
+                    b[:, DR * j : DR * (j + 1)],
+                    wk[:, DQ * h + DN : DQ * (h + 1)],
+                    sk[:, DQ * h + DN : DQ * (h + 1)],
                 )
 
-        def ev_r(i, half, add_engine="g"):
+        def ev_r(i, half, add_engine="v"):
             r = banks["r", i, half][:].rearrange("p (h a j) -> p h a j", a=2, j=32)
             rc = rot.tile([P, 8, 2, 32], F32)
             rs = rot.tile([P, 8, 2, 32], F32)
@@ -296,172 +298,173 @@ def tile_fa3mlaattention_pa_w8_kernel(
             hs = slice(8 * h0, 8 * h1)
             nc.sync.dma_start(out=k_rows[i // 2][:, i % 2, hs, :], in_=ko[i][:, hs, :])
 
+        turn_scale()
+        cast(0, 3, 4, "v")
         cast(0, 0, 1, "v")
         cast(0, 1, 2)
-        turn_x(0, 0)
-        cast(0, 3, 4)
-        cast(0, 2, 3, "v")
-        product_x(0, 0)
-        product_x(0, 1)
-        turn_x(0, 1)
-        cast(1, 0, 2)
-        product_x(0, 2)
-        quantise_x(0, 0)
-        turn_x(1, 0)
-        product_x(0, 3)
-        down(0, 0)
-        quantise_x(0, 1)
         cast(1, 2, 4)
-        down(0, 1)
-        product_x(1, 1)
+        cast(1, 0, 2, "v")
+        copy_scale()
+        turn_x(1, 0)
+        cast(2, 2, 4)
         turn_x(1, 1)
+        cast(0, 2, 3, "v")
         product_x(1, 0)
+        product_x(1, 1)
+        cast(2, 0, 2)
+        turn_x(0, 1)
         product_x(1, 2)
-        quantise_x(1, 0)
-        round_kv(0, 1, 2)
-        round_kv(0, 0, 1)
-        turn_kv(0)
-        down(1, 0)
-        gather_kv(0, "s")
         product_x(1, 3)
-        quantise_kv(0)
+        turn_x(0, 0)
+        quantise_x(1, 0)
         quantise_x(1, 1)
-        mm_v(0, 0)
+        product_x(0, 0)
+        down(1, 0)
         down(1, 1)
+        turn_x(2, 1)
+        round_kv(1, 0, 2)
+        product_x(0, 1)
+        product_x(0, 2)
+        product_x(0, 3)
+        turn_x(2, 0)
+        turn_kv(1)
+        quantise_x(0, 0)
+        quantise_x(0, 1)
+        down(0, 0)
+        gather_kv(1, "s")
+        product_x(2, 1)
+        down(0, 1)
+        quantise_kv(1)
+        product_x(2, 0)
+        round_kv(0, 1, 2, "v")
+        mm_v(1, 2)
+        round_kv(0, 0, 1)
+        mm_v(1, 3)
+        turn_kv(0)
+        begin_out(1)
+        ev_v(1, 2)
+        mm_v(1, 1)
+        ev_v(1, 3)
+        store_v(1, 2, 4)
+        mm_v(1, 0)
+        product_x(2, 2)
+        quantise_x(2, 0)
+        product_x(2, 3)
+        gather_kv(0, "s")
+        quantise_kv(0)
+        ev_v(1, 1)
+        cast(3, 2, 4, "v")
+        down(2, 0)
+        ev_v(1, 0)
+        store_v(1, 0, 2)
         cast(3, 0, 2, "v")
+        mm_v(0, 0)
         begin_out(0)
         ev_v(0, 0)
         store_v(0, 0, 1)
         mm_v(0, 1)
-        turn_x(3, 0)
-        round_kv(1, 0, 2)
-        cast(2, 0, 2, "v")
-        turn_kv(1)
-        mm_v(0, 2)
-        cast(3, 2, 4, "v")
         ev_v(0, 1)
         store_v(0, 1, 2)
-        gather_rope_scales()
-        mm_v(0, 3)
-        product_x(3, 0)
-        gather_kv(1, "s")
-        turn_x(3, 1)
-        quantise_kv(1)
-        product_x(3, 1)
-        product_x(3, 2)
-        ev_v(0, 2)
-        ev_v(0, 3)
-        store_v(0, 2, 4)
-        mm_v(1, 0)
-        mm_v(1, 1)
-        mm_v(1, 3)
-        begin_out(1)
-        ev_v(1, 0)
-        gather_rope_weights(1)
-        ev_v(1, 1)
-        store_v(1, 0, 2)
-        ev_v(1, 3)
-        mm_r(1, 1)
-        product_x(3, 3)
-        mm_n(1, 3)
-        mm_v(1, 2)
-        ev_v(1, 2)
-        store_v(1, 2, 4)
-        mm_r(0, 1)
-        mm_n(1, 2)
-        mm_n(1, 0)
-        mm_n(0, 3)
-        ev_n(1, 2)
-        ev_n(1, 3)
-        ev_r(1, 1)
-        store_k(1, 1, 2)
-        gather_rope_weights(0)
-        mm_n(0, 0)
-        ev_r(0, 1)
-        quantise_x(3, 0)
-        mm_r(0, 0)
-        mm_n(0, 2)
-        mm_n(0, 1)
-        quantise_x(3, 1)
-        ev_n(0, 3)
         mm_r(1, 0)
-        down(3, 0)
-        ev_n(0, 2)
-        store_k(0, 1, 2)
-        ev_r(0, 0)
-        down(3, 1)
-        ev_n(0, 1)
+        quantise_x(2, 1)
         mm_n(1, 1)
-        turn_x(2, 0)
+        ev_n(1, 1)
+        mm_n(1, 0)
+        ev_n(1, 0)
+        ev_r(1, 0)
+        store_k(1, 0, 1)
+        down(2, 1)
+        mm_r(0, 0)
+        round_kv(2, 0, 2)
+        mm_n(0, 1)
+        ev_r(0, 0)
+        mm_v(0, 3)
+        mm_n(0, 0)
+        turn_kv(2)
+        turn_x(3, 1)
+        turn_x(3, 0)
+        ev_n(0, 1)
         ev_n(0, 0)
         store_k(0, 0, 1)
-        ev_r(1, 0)
+        gather_kv(2, "s")
+        quantise_kv(2)
+        ev_v(0, 3)
+        product_x(3, 2)
+        product_x(3, 0)
+        mm_v(0, 2)
+        ev_v(0, 2)
+        store_v(0, 2, 4)
+        mm_v(2, 2)
+        mm_v(2, 0)
+        product_x(3, 1)
+        product_x(3, 3)
+        mm_v(2, 3)
+        mm_v(2, 1)
+        quantise_x(3, 0)
+        mm_n(1, 3)
+        begin_out(2)
+        ev_v(2, 0)
+        ev_v(2, 1)
+        store_v(2, 0, 2)
+        mm_r(1, 1)
+        mm_n(1, 2)
+        down(3, 0)
+        ev_v(2, 3)
+        ev_v(2, 2)
+        store_v(2, 2, 4)
+        quantise_x(3, 1)
+        down(3, 1)
+        ev_n(1, 2)
+        ev_n(1, 3)
+        mm_r(0, 1)
+        mm_n(0, 2)
         round_kv(3, 0, 2)
-        cast(2, 2, 4)
-        product_x(2, 0)
+        ev_n(0, 2)
+        mm_n(2, 3)
+        mm_n(0, 3)
+        ev_n(0, 3)
         turn_kv(3)
         gather_kv(3, "s")
-        ev_n(1, 0)
+        ev_n(2, 3)
+        ev_r(1, 1)
+        store_k(1, 1, 2)
+        mm_n(2, 1)
+        ev_n(2, 1)
+        mm_r(2, 1)
+        ev_r(0, 1)
+        store_k(0, 1, 2)
         quantise_kv(3)
-        turn_x(2, 1)
-        mm_v(3, 0)
-        mm_r(3, 0)
-        mm_v(3, 1)
-        ev_n(1, 1)
-        store_k(1, 0, 1)
-        product_x(2, 1)
         mm_v(3, 3)
-        product_x(2, 2)
-        product_x(2, 3)
         mm_v(3, 2)
-        quantise_x(2, 0)
+        mm_v(3, 1)
         begin_out(3)
-        ev_v(3, 0)
-        ev_v(3, 1)
-        store_v(3, 0, 2)
-        quantise_x(2, 1)
-        mm_r(3, 1)
-        mm_n(3, 1)
+        ev_v(3, 3, "v")
+        mm_v(3, 0)
+        mm_r(2, 0)
         ev_v(3, 2)
-        down(2, 0)
-        ev_v(3, 3)
         store_v(3, 2, 4)
-        ev_n(3, 1)
-        down(2, 1)
-        mm_n(3, 0)
-        round_kv(2, 0, 2)
+        ev_r(2, 1, "g")
+        ev_r(2, 0, "g")
+        mm_n(2, 2)
         mm_n(3, 2)
-        turn_kv(2)
+        ev_v(3, 1)
+        ev_v(3, 0)
+        store_v(3, 0, 2)
+        mm_r(3, 0)
+        ev_r(3, 0, "g")
         mm_n(3, 3)
-        ev_r(3, 0)
+        mm_r(3, 1)
+        mm_n(2, 0)
+        ev_n(2, 2)
+        store_k(2, 1, 2)
+        ev_n(3, 2)
         ev_r(3, 1)
+        ev_n(3, 3)
+        mm_n(3, 1)
+        ev_n(2, 0)
+        store_k(2, 0, 1)
+        mm_n(3, 0)
+        ev_n(3, 1)
         ev_n(3, 0)
         store_k(3, 0, 1)
-        gather_kv(2)
-        quantise_kv(2)
-        ev_n(3, 2, "v")
-        mm_v(2, 1)
-        mm_r(2, 0)
-        begin_out(2)
-        ev_r(2, 0)
-        mm_v(2, 2)
-        ev_n(3, 3)
         store_k(3, 1, 2)
-        ev_v(2, 1)
-        mm_v(2, 3)
-        mm_v(2, 0)
-        mm_n(2, 0)
-        ev_v(2, 0, "v")
-        ev_v(2, 2)
-        mm_r(2, 1)
-        mm_n(2, 2)
-        mm_n(2, 3)
-        ev_v(2, 3)
-        store_v(2, 0, 4)
-        mm_n(2, 1)
-        ev_n(2, 0)
-        ev_n(2, 2)
-        ev_n(2, 3)
-        ev_n(2, 1)
-        ev_r(2, 1, "v")
-        store_k(2, 0, 2)

@@ -47,15 +47,17 @@ def tile_fa3mlaattention_pa_w8_kernel(
         psum = ctx.enter_context(tc.psum_pool(name="psum", bufs=8))
         ctx.enter_context(tc.manual_schedule())
 
-        def bank():
+        def bank(warm_ups=0):
             b = psum.tile([P, 512], F32, name="bank", tag="bank")
+            for j in range(warm_ups):
+                nc.tensor.matmul(b[:], lhsT=warm[:, 0:P], rhs=warm[:], start=True, stop=True)
             return b
 
         sd = keep.tile([P, R], U8, align_bytes=64)
         sv = keep.tile([P, 512], U8, align_bytes=64)
         sk = keep.tile([P, H * DQ], U8, align_bytes=64)
-        xs_rows = keep.tile([P, K_PASS], F32)
-        nc.vector.memset(xs_rows[:], 0.0)
+        warm = keep.tile([P, 512], BF16)
+        nc.vector.memset(warm[:], 0.0)
         for plane in (sd, sv):
             nc.vector.memset(plane[:].bitcast(I32), 0)
 
@@ -81,17 +83,13 @@ def tile_fa3mlaattention_pa_w8_kernel(
                 nc.sync.dma_start(out=plane[32 * q : 32 * q + parts, :].bitcast(I32), in_=rows_of_quadrant(q).bitcast(I32))
 
         load_x(0, 0, C)
-        nc.sync.dma_start(out=xs_rows[0:G, :], in_=x_scale.rearrange("o q (g k) -> (o q g) k", g=G))
+        nc.sync.dma_start(out=xs[:], in_=x_scale.rearrange("o q (g p t) -> p (o q g) t", p=P, t=4))
         load_scales(sd, lambda q: w_kv_down_scales[:, 4 * q : 4 * q + 4, :])
         load_x(1, 0, C)
-        for g in (0, 2):
-            nc.sync.dma_start(
-                out=wd[:, g : g + 2, :],
-                in_=w_kv_down_words[g : g + 2].rearrange("g p n t -> p g (n t)").bitcast(I32),
-            )
-        load_x(2, 0, C)
+        nc.sync.dma_start(out=wd[:], in_=w_kv_down_words.rearrange("g p n t -> p g (n t)").bitcast(I32))
         nc.sync.dma_start(out=wv[:], in_=w_v_up_words[0].rearrange("p n t -> p (n t)").bitcast(I32))
         load_scales(sv, lambda q: w_v_up_scales[0, 4 * q : 4 * q + 4, :].rearrange("r (c n) -> c r n", c=4))
+        load_x(2, 0, C)
         nc.sync.dma_start(out=wk[:], in_=w_k_up_words[0].rearrange("p n t -> p (n t)").bitcast(I32))
         load_scales(sk, lambda q: w_k_up_scales[0, 4 * q : 4 * q + 4, :], parts=4)
         load_x(3, 0, C)
@@ -109,17 +107,6 @@ def tile_fa3mlaattention_pa_w8_kernel(
 
         make_tables()
 
-        xs_bank = []
-
-        def turn_scale():
-            t = bank()
-            xs_bank.append(t)
-            for j in range(4):
-                nc.tensor.transpose(t[:, P * j : P * (j + 1)], xs_rows[:, j::4], ident[:])
-
-        def copy_scale():
-            nc.vector.tensor_copy(out=xs[:], in_=xs_bank[0][:].rearrange("p (t r) -> p r t", t=4)[:, 0:G, :])
-
         xb, xq, xqs, acc, kvw, kvq, kvs, ko, vo = ({} for n in range(9))
 
         def cast(i, a, b, engine="s"):
@@ -136,7 +123,7 @@ def tile_fa3mlaattention_pa_w8_kernel(
 
         def turn_x(i, half):
             words = xb[i][:].bitcast(F32)
-            t = bank()
+            t = bank((6, 1, 1, 1)[2 * i + half] if i < 2 else 0)
             xt[i, half] = t
             for j in range(4):
                 g, u = 2 * half + j // 2, j % 2
@@ -199,7 +186,7 @@ def tile_fa3mlaattention_pa_w8_kernel(
             copy_out(engine, kvw[i][:, 256 * a : 256 * b], acc[i][:, 256 * a : 256 * b])
 
         def turn_kv(i):
-            t = bank()
+            t = bank(2 if i == 0 else 0)
             xt[i, "kv"] = t
             words = kvw[i][:].bitcast(F32)
             for u in range(2):
@@ -298,173 +285,171 @@ def tile_fa3mlaattention_pa_w8_kernel(
             hs = slice(8 * h0, 8 * h1)
             nc.sync.dma_start(out=k_rows[i // 2][:, i % 2, hs, :], in_=ko[i][:, hs, :])
 
-        turn_scale()
-        cast(0, 3, 4, "v")
         cast(0, 0, 1, "v")
-        cast(0, 1, 2)
-        cast(1, 2, 4)
-        cast(1, 0, 2, "v")
-        copy_scale()
-        turn_x(1, 0)
-        cast(2, 2, 4)
-        turn_x(1, 1)
-        cast(0, 2, 3, "v")
-        product_x(1, 0)
-        product_x(1, 1)
-        cast(2, 0, 2)
-        turn_x(0, 1)
-        product_x(1, 2)
-        product_x(1, 3)
+        cast(0, 2, 3)
+        cast(0, 3, 4)
+        cast(0, 1, 2, "v")
         turn_x(0, 0)
-        quantise_x(1, 0)
-        quantise_x(1, 1)
+        cast(1, 0, 2)
+        turn_x(0, 1)
         product_x(0, 0)
-        down(1, 0)
-        down(1, 1)
-        turn_x(2, 1)
-        round_kv(1, 0, 2)
         product_x(0, 1)
         product_x(0, 2)
         product_x(0, 3)
-        turn_x(2, 0)
-        turn_kv(1)
         quantise_x(0, 0)
-        quantise_x(0, 1)
+        turn_x(1, 0)
+        cast(1, 2, 4)
+        turn_x(1, 1)
         down(0, 0)
-        gather_kv(1, "s")
-        product_x(2, 1)
+        quantise_x(0, 1)
+        product_x(1, 0)
+        product_x(1, 1)
         down(0, 1)
-        quantise_kv(1)
-        product_x(2, 0)
-        round_kv(0, 1, 2, "v")
-        mm_v(1, 2)
-        round_kv(0, 0, 1)
-        mm_v(1, 3)
+        product_x(1, 2)
+        quantise_x(1, 0)
+        round_kv(0, 1, 2)
+        round_kv(0, 0, 1, "v")
         turn_kv(0)
-        begin_out(1)
-        ev_v(1, 2)
-        mm_v(1, 1)
-        ev_v(1, 3)
-        store_v(1, 2, 4)
-        mm_v(1, 0)
-        product_x(2, 2)
-        quantise_x(2, 0)
-        product_x(2, 3)
+        product_x(1, 3)
+        down(1, 0)
         gather_kv(0, "s")
+        quantise_x(1, 1)
         quantise_kv(0)
-        ev_v(1, 1)
-        cast(3, 2, 4, "v")
-        down(2, 0)
-        ev_v(1, 0)
-        store_v(1, 0, 2)
-        cast(3, 0, 2, "v")
-        mm_v(0, 0)
-        begin_out(0)
-        ev_v(0, 0)
-        store_v(0, 0, 1)
-        mm_v(0, 1)
-        ev_v(0, 1)
-        store_v(0, 1, 2)
-        mm_r(1, 0)
-        quantise_x(2, 1)
-        mm_n(1, 1)
-        ev_n(1, 1)
-        mm_n(1, 0)
-        ev_n(1, 0)
-        ev_r(1, 0)
-        store_k(1, 0, 1)
-        down(2, 1)
-        mm_r(0, 0)
-        round_kv(2, 0, 2)
-        mm_n(0, 1)
-        ev_r(0, 0)
+        cast(2, 2, 4, "v")
+        down(1, 1)
+        cast(2, 0, 2)
+        round_kv(1, 0, 2)
         mm_v(0, 3)
-        mm_n(0, 0)
-        turn_kv(2)
-        turn_x(3, 1)
-        turn_x(3, 0)
-        ev_n(0, 1)
-        ev_n(0, 0)
-        store_k(0, 0, 1)
-        gather_kv(2, "s")
-        quantise_kv(2)
-        ev_v(0, 3)
-        product_x(3, 2)
-        product_x(3, 0)
         mm_v(0, 2)
+        begin_out(0)
+        ev_v(0, 3, "v")
+        turn_x(2, 1)
         ev_v(0, 2)
         store_v(0, 2, 4)
-        mm_v(2, 2)
-        mm_v(2, 0)
-        product_x(3, 1)
-        product_x(3, 3)
-        mm_v(2, 3)
-        mm_v(2, 1)
-        quantise_x(3, 0)
+        turn_kv(1)
+        gather_kv(1, "s")
+        mm_v(0, 0)
+        product_x(2, 2)
+        mm_v(0, 1)
+        product_x(2, 3)
+        quantise_kv(1)
+        turn_x(2, 0)
+        ev_v(0, 0)
+        store_v(0, 0, 1)
+        mm_v(1, 1)
+        mm_v(1, 2)
+        quantise_x(2, 1)
+        product_x(2, 0)
+        ev_v(0, 1)
+        store_v(0, 1, 2)
+        mm_v(1, 0)
+        begin_out(1)
+        ev_v(1, 1)
+        ev_v(1, 0)
+        store_v(1, 0, 2)
+        mm_v(1, 3)
+        mm_r(1, 0)
+        product_x(2, 1)
+        mm_n(1, 1)
+        cast(3, 2, 4, "v")
+        quantise_x(2, 0)
+        mm_n(1, 0)
         mm_n(1, 3)
-        begin_out(2)
-        ev_v(2, 0)
-        ev_v(2, 1)
-        store_v(2, 0, 2)
+        ev_v(1, 2)
+        ev_v(1, 3)
+        store_v(1, 2, 4)
         mm_r(1, 1)
         mm_n(1, 2)
-        down(3, 0)
+        down(2, 0)
+        ev_r(1, 0)
+        ev_n(1, 1)
+        down(2, 1)
+        ev_n(1, 0)
+        store_k(1, 0, 1)
+        mm_r(0, 0)
+        ev_r(1, 1)
+        ev_n(1, 3)
+        mm_n(0, 0)
+        mm_n(0, 1)
+        ev_n(1, 2)
+        store_k(1, 1, 2)
+        round_kv(2, 0, 2)
+        cast(3, 0, 2)
+        turn_kv(2)
+        turn_x(3, 1)
+        ev_r(0, 0)
+        gather_kv(2, "s")
+        turn_x(3, 0)
+        quantise_kv(2)
+        mm_n(0, 2)
+        product_x(3, 2)
+        product_x(3, 0)
+        mm_v(2, 3)
+        product_x(3, 1)
+        mm_v(2, 2)
+        ev_n(0, 0)
+        mm_v(2, 1)
+        ev_n(0, 1)
+        store_k(0, 0, 1)
+        product_x(3, 3)
+        mm_v(2, 0)
+        mm_n(2, 0)
+        begin_out(2)
         ev_v(2, 3)
+        mm_n(0, 3)
         ev_v(2, 2)
         store_v(2, 2, 4)
-        quantise_x(3, 1)
-        down(3, 1)
-        ev_n(1, 2)
-        ev_n(1, 3)
+        ev_v(2, 0)
+        quantise_x(3, 0)
         mm_r(0, 1)
-        mm_n(0, 2)
-        round_kv(3, 0, 2)
-        ev_n(0, 2)
-        mm_n(2, 3)
-        mm_n(0, 3)
+        down(3, 0)
+        ev_v(2, 1)
+        store_v(2, 0, 2)
+        quantise_x(3, 1)
+        ev_r(0, 1)
+        down(3, 1)
         ev_n(0, 3)
+        mm_r(2, 0)
+        ev_n(0, 2)
+        store_k(0, 1, 2)
+        round_kv(3, 0, 2)
+        ev_n(2, 0)
+        mm_n(2, 1)
+        mm_n(2, 2)
+        ev_n(2, 1)
         turn_kv(3)
         gather_kv(3, "s")
-        ev_n(2, 3)
-        ev_r(1, 1)
-        store_k(1, 1, 2)
-        mm_n(2, 1)
-        ev_n(2, 1)
-        mm_r(2, 1)
-        ev_r(0, 1)
-        store_k(0, 1, 2)
+        ev_r(2, 0)
+        store_k(2, 0, 1)
         quantise_kv(3)
-        mm_v(3, 3)
+        mm_n(2, 3)
+        mm_r(2, 1)
+        ev_n(2, 2)
         mm_v(3, 2)
+        mm_v(3, 3)
+        mm_v(3, 0)
+        ev_n(2, 3)
         mm_v(3, 1)
         begin_out(3)
-        ev_v(3, 3, "v")
-        mm_v(3, 0)
-        mm_r(2, 0)
-        ev_v(3, 2)
+        ev_v(3, 3)
+        mm_r(3, 1)
+        ev_v(3, 2, "v")
         store_v(3, 2, 4)
-        ev_r(2, 1, "g")
-        ev_r(2, 0, "g")
-        mm_n(2, 2)
-        mm_n(3, 2)
         ev_v(3, 1)
         ev_v(3, 0)
         store_v(3, 0, 2)
-        mm_r(3, 0)
-        ev_r(3, 0, "g")
-        mm_n(3, 3)
-        mm_r(3, 1)
-        mm_n(2, 0)
-        ev_n(2, 2)
-        store_k(2, 1, 2)
-        ev_n(3, 2)
-        ev_r(3, 1)
-        ev_n(3, 3)
         mm_n(3, 1)
-        ev_n(2, 0)
-        store_k(2, 0, 1)
+        mm_n(3, 3)
+        mm_r(3, 0)
+        ev_r(2, 1, "g")
+        store_k(2, 1, 2)
+        ev_r(3, 1, "g")
+        ev_r(3, 0)
+        mm_n(3, 2)
+        ev_n(3, 3)
         mm_n(3, 0)
         ev_n(3, 1)
+        ev_n(3, 2)
+        store_k(3, 1, 2)
         ev_n(3, 0)
         store_k(3, 0, 1)
-        store_k(3, 1, 2)

@@ -36,9 +36,9 @@ def tile_fa3mlaattention_pa_w8_kernel(
     out_v,
 ):
     nc = tc.nc
-    x_rows = x_bytes.rearrange("b (p j) k -> b p j k", p=P)
-    k_rows = out_k.rearrange("b (p j) h d -> b p j h d", p=P)
-    v_rows = out_v.rearrange("b (p j) h d -> b p j (h d)", p=P)
+    x_rows = x_bytes.rearrange("b (j p) k -> b p j k", p=P)
+    k_rows = out_k.rearrange("b (j p) h d -> b p j h d", p=P)
+    v_rows = out_v.rearrange("b (j p) h d -> b p j (h d)", p=P)
 
     with ExitStack() as ctx:
         keep = ctx.enter_context(tc.tile_pool(name="keep", bufs=1))
@@ -94,7 +94,7 @@ def tile_fa3mlaattention_pa_w8_kernel(
         load_scales(sk, lambda q: w_k_up_scales[0, 4 * q : 4 * q + 4, :], parts=4)
         load_x(3, 0, C)
         cs = keep.tile([P, 2, DR], BF16)
-        nc.gpsimd.dma_start(out=cs[:], in_=freqs_cis.rearrange("(p c) j e -> p c (j e)", p=P))
+        nc.gpsimd.dma_start(out=cs[:], in_=freqs_cis.rearrange("(c p) j e -> p c (j e)", p=P))
 
         cos = keep.tile([P, 2, 2, 32], F32)
         sin = keep.tile([P, 2, 2, 32], F32)
@@ -123,7 +123,7 @@ def tile_fa3mlaattention_pa_w8_kernel(
 
         def turn_x(i, half):
             words = xb[i][:].bitcast(F32)
-            t = bank((6, 1, 1, 1)[2 * i + half] if i < 2 else 0)
+            t = bank((6, 1)[half] if i == 0 else 0)
             xt[i, half] = t
             for j in range(4):
                 g, u = 2 * half + j // 2, j % 2
@@ -186,7 +186,7 @@ def tile_fa3mlaattention_pa_w8_kernel(
             copy_out(engine, kvw[i][:, 256 * a : 256 * b], acc[i][:, 256 * a : 256 * b])
 
         def turn_kv(i):
-            t = bank(2 if i == 0 else 0)
+            t = bank()
             xt[i, "kv"] = t
             words = kvw[i][:].bitcast(F32)
             for u in range(2):
@@ -286,170 +286,168 @@ def tile_fa3mlaattention_pa_w8_kernel(
             nc.sync.dma_start(out=k_rows[i // 2][:, i % 2, hs, :], in_=ko[i][:, hs, :])
 
         cast(0, 0, 1, "v")
-        cast(0, 2, 3)
-        cast(0, 3, 4)
         cast(0, 1, 2, "v")
         turn_x(0, 0)
-        cast(1, 0, 2)
-        turn_x(0, 1)
+        cast(0, 3, 4, "v")
+        cast(0, 2, 3)
         product_x(0, 0)
         product_x(0, 1)
+        turn_x(0, 1)
+        cast(1, 0, 2)
         product_x(0, 2)
-        product_x(0, 3)
+        cast(1, 2, 4)
         quantise_x(0, 0)
         turn_x(1, 0)
-        cast(1, 2, 4)
-        turn_x(1, 1)
+        product_x(0, 3)
+        product_x(1, 1)
         down(0, 0)
         quantise_x(0, 1)
-        product_x(1, 0)
-        product_x(1, 1)
+        turn_x(1, 1)
         down(0, 1)
+        round_kv(0, 0, 1)
+        product_x(1, 0)
         product_x(1, 2)
-        quantise_x(1, 0)
         round_kv(0, 1, 2)
-        round_kv(0, 0, 1, "v")
-        turn_kv(0)
+        quantise_x(1, 0)
+        cast(2, 2, 4)
         product_x(1, 3)
-        down(1, 0)
-        gather_kv(0, "s")
         quantise_x(1, 1)
-        quantise_kv(0)
-        cast(2, 2, 4, "v")
+        cast(2, 0, 2, "v")
+        down(1, 0)
+        turn_kv(0)
         down(1, 1)
-        cast(2, 0, 2)
-        round_kv(1, 0, 2)
-        mm_v(0, 3)
-        mm_v(0, 2)
-        begin_out(0)
-        ev_v(0, 3, "v")
-        turn_x(2, 1)
-        ev_v(0, 2)
-        store_v(0, 2, 4)
-        turn_kv(1)
-        gather_kv(1, "s")
-        mm_v(0, 0)
-        product_x(2, 2)
-        mm_v(0, 1)
-        product_x(2, 3)
-        quantise_kv(1)
+        gather_kv(0)
         turn_x(2, 0)
+        round_kv(1, 0, 2)
+        turn_x(2, 1)
+        quantise_kv(0)
+        turn_kv(1)
+        product_x(2, 0)
+        product_x(2, 1)
+        product_x(2, 3)
+        mm_v(0, 0)
+        gather_kv(1, "s")
+        mm_v(0, 1)
+        begin_out(0)
         ev_v(0, 0)
         store_v(0, 0, 1)
+        mm_v(0, 2)
+        mm_v(0, 3)
+        quantise_kv(1)
+        mm_v(1, 0)
         mm_v(1, 1)
+        mm_v(1, 3)
         mm_v(1, 2)
-        quantise_x(2, 1)
-        product_x(2, 0)
+        quantise_x(2, 0)
         ev_v(0, 1)
         store_v(0, 1, 2)
-        mm_v(1, 0)
+        ev_v(0, 3)
+        ev_v(0, 2, "v")
+        store_v(0, 2, 4)
+        down(2, 0)
+        product_x(2, 2)
         begin_out(1)
         ev_v(1, 1)
-        ev_v(1, 0)
-        store_v(1, 0, 2)
-        mm_v(1, 3)
-        mm_r(1, 0)
-        product_x(2, 1)
-        mm_n(1, 1)
-        cast(3, 2, 4, "v")
-        quantise_x(2, 0)
-        mm_n(1, 0)
-        mm_n(1, 3)
+        mm_r(0, 1)
+        cast(3, 0, 2, "v")
+        mm_n(0, 3)
         ev_v(1, 2)
-        ev_v(1, 3)
-        store_v(1, 2, 4)
+        ev_v(1, 0)
+        ev_v(1, 3, "v")
+        store_v(1, 0, 4)
+        quantise_x(2, 1)
+        ev_r(0, 1, "g")
+        mm_r(1, 0)
+        mm_n(0, 2)
+        cast(3, 2, 4)
+        mm_n(1, 0)
         mm_r(1, 1)
-        mm_n(1, 2)
-        down(2, 0)
-        ev_r(1, 0)
-        ev_n(1, 1)
-        down(2, 1)
+        ev_n(0, 3)
         ev_n(1, 0)
-        store_k(1, 0, 1)
+        down(2, 1)
+        mm_n(1, 2)
+        mm_n(1, 1)
         mm_r(0, 0)
-        ev_r(1, 1)
+        mm_n(1, 3)
+        round_kv(2, 0, 2)
+        ev_n(1, 1)
+        ev_n(0, 2, "v")
+        store_k(0, 1, 2)
+        turn_kv(2)
+        ev_r(1, 0, "g")
+        store_k(1, 0, 1)
+        gather_kv(2, "s")
+        ev_r(1, 1, "g")
+        ev_r(0, 0, "g")
+        turn_x(3, 0)
         ev_n(1, 3)
-        mm_n(0, 0)
+        turn_x(3, 1)
         mm_n(0, 1)
         ev_n(1, 2)
         store_k(1, 1, 2)
-        round_kv(2, 0, 2)
-        cast(3, 0, 2)
-        turn_kv(2)
-        turn_x(3, 1)
-        ev_r(0, 0)
-        gather_kv(2, "s")
-        turn_x(3, 0)
+        mm_n(0, 0)
         quantise_kv(2)
-        mm_n(0, 2)
-        product_x(3, 2)
-        product_x(3, 0)
-        mm_v(2, 3)
-        product_x(3, 1)
-        mm_v(2, 2)
-        ev_n(0, 0)
-        mm_v(2, 1)
         ev_n(0, 1)
-        store_k(0, 0, 1)
+        product_x(3, 0)
+        product_x(3, 1)
         product_x(3, 3)
+        mm_v(2, 3)
+        mm_v(2, 2)
+        mm_r(2, 0)
+        ev_n(0, 0)
+        store_k(0, 0, 1)
+        mm_v(2, 1)
         mm_v(2, 0)
-        mm_n(2, 0)
         begin_out(2)
         ev_v(2, 3)
-        mm_n(0, 3)
-        ev_v(2, 2)
-        store_v(2, 2, 4)
-        ev_v(2, 0)
+        product_x(3, 2)
         quantise_x(3, 0)
-        mm_r(0, 1)
         down(3, 0)
-        ev_v(2, 1)
-        store_v(2, 0, 2)
         quantise_x(3, 1)
-        ev_r(0, 1)
         down(3, 1)
-        ev_n(0, 3)
-        mm_r(2, 0)
-        ev_n(0, 2)
-        store_k(0, 1, 2)
-        round_kv(3, 0, 2)
-        ev_n(2, 0)
+        mm_n(2, 0)
         mm_n(2, 1)
-        mm_n(2, 2)
-        ev_n(2, 1)
-        turn_kv(3)
-        gather_kv(3, "s")
-        ev_r(2, 0)
-        store_k(2, 0, 1)
-        quantise_kv(3)
         mm_n(2, 3)
+        ev_v(2, 2)
+        ev_v(2, 1)
+        ev_v(2, 0, "v")
+        store_v(2, 0, 4)
+        ev_r(2, 0)
+        round_kv(3, 0, 2)
+        turn_kv(3)
+        gather_kv(3)
+        quantise_kv(3)
         mm_r(2, 1)
-        ev_n(2, 2)
-        mm_v(3, 2)
+        ev_n(2, 0)
+        ev_n(2, 1)
+        store_k(2, 0, 1)
         mm_v(3, 3)
+        mm_v(3, 2)
         mm_v(3, 0)
-        ev_n(2, 3)
         mm_v(3, 1)
         begin_out(3)
-        ev_v(3, 3)
-        mm_r(3, 1)
-        ev_v(3, 2, "v")
-        store_v(3, 2, 4)
-        ev_v(3, 1)
-        ev_v(3, 0)
-        store_v(3, 0, 2)
-        mm_n(3, 1)
-        mm_n(3, 3)
+        ev_v(3, 2)
+        ev_n(2, 3, "v")
         mm_r(3, 0)
+        mm_n(3, 0)
+        mm_n(2, 2)
+        mm_r(3, 1)
+        ev_v(3, 0)
+        ev_v(3, 3, "v")
+        store_v(3, 2, 4)
+        mm_n(3, 1)
+        ev_v(3, 1)
+        store_v(3, 0, 2)
+        ev_n(3, 0)
+        ev_n(2, 2)
+        ev_n(3, 1)
+        mm_n(3, 2)
+        mm_n(3, 3)
         ev_r(2, 1, "g")
         store_k(2, 1, 2)
-        ev_r(3, 1, "g")
-        ev_r(3, 0)
-        mm_n(3, 2)
-        ev_n(3, 3)
-        mm_n(3, 0)
-        ev_n(3, 1)
-        ev_n(3, 2)
-        store_k(3, 1, 2)
-        ev_n(3, 0)
+        ev_r(3, 0, "g")
         store_k(3, 0, 1)
+        ev_r(3, 1)
+        ev_n(3, 2)
+        ev_n(3, 3)
+        store_k(3, 1, 2)

from contextlib import ExitStack

import concourse.mybir as mybir
from concourse.masks import make_identity

F32 = mybir.dt.float32
BF16 = mybir.dt.bfloat16
I32 = mybir.dt.int32
U8 = mybir.dt.uint8
E4M3 = mybir.dt.float8_e4m3fn
E4M3X4 = mybir.dt.float8_e4m3fn_x4
MULT = mybir.AluOpType.mult
ADD = mybir.AluOpType.add

B, T, C, R, H, DN, DR, DV = 2, 256, 2048, 512, 16, 128, 64, 128
DQ = DN + DR
P = 128
K_PASS = 512
G = C // K_PASS
TILES = B * T // P
FLOPS = 2 * B * T * (C * R + R * H * (DQ + DV))


def tile_fa3mlaattention_pa_w8_kernel(
    tc,
    x_bytes,
    x_scale,
    freqs_cis,
    w_kv_down_words,
    w_kv_down_scales,
    w_k_up_words,
    w_k_up_scales,
    w_v_up_words,
    w_v_up_scales,
    out_k,
    out_v,
):
    nc = tc.nc
    x_rows = x_bytes.rearrange("b (j p) k -> b p j k", p=P)
    k_rows = out_k.rearrange("b (j p) h d -> b p j h d", p=P)
    v_rows = out_v.rearrange("b (j p) h d -> b p j (h d)", p=P)

    with ExitStack() as ctx:
        keep = ctx.enter_context(tc.tile_pool(name="keep", bufs=1))
        tok = ctx.enter_context(tc.tile_pool(name="tok", bufs=TILES))
        rot = ctx.enter_context(tc.tile_pool(name="rot", bufs=8))
        psum = ctx.enter_context(tc.psum_pool(name="psum", bufs=8))
        ctx.enter_context(tc.manual_schedule())

        def bank(warm_ups=0):
            b = psum.tile([P, 512], F32, name="bank", tag="bank")
            for j in range(warm_ups):
                nc.tensor.matmul(b[:], lhsT=warm[:, 0:P], rhs=warm[:], start=True, stop=True)
            return b

        sd = keep.tile([P, R], U8, align_bytes=64)
        sv = keep.tile([P, 512], U8, align_bytes=64)
        sk = keep.tile([P, H * DQ], U8, align_bytes=64)
        warm = keep.tile([P, 512], BF16)
        nc.vector.memset(warm[:], 0.0)
        for plane in (sd, sv):
            nc.vector.memset(plane[:].bitcast(I32), 0)

        ident = keep.tile([P, P], F32)
        make_identity(nc, ident[:])
        nc.gpsimd.memset(sk[:].bitcast(I32), 0)
        wd = keep.tile([P, G, R], I32, align_bytes=64)
        wv = keep.tile([P, H * DV], I32, align_bytes=64)
        wk = keep.tile([P, H * DQ], I32, align_bytes=64)

        x_pair = []
        for b in range(B):
            x_u8 = keep.tile([P, 2, C], U8, align_bytes=64, name="x_u8_%d" % b)
            x_pair.append(x_u8)
        xs = keep.tile([P, G, 4], F32)
        xu = [x_pair[i // 2][:, i % 2, :] for i in range(TILES)]

        def load_x(i, a, b):
            nc.sync.dma_start(out=xu[i][:, a:b], in_=x_rows[i // 2][:, i % 2, a:b])

        def load_scales(plane, rows_of_quadrant, parts=16):
            for q in range(4):
                nc.sync.dma_start(out=plane[32 * q : 32 * q + parts, :].bitcast(I32), in_=rows_of_quadrant(q).bitcast(I32))

        load_x(0, 0, C)
        nc.sync.dma_start(out=xs[:], in_=x_scale.rearrange("o q (g p t) -> p (o q g) t", p=P, t=4))
        load_scales(sd, lambda q: w_kv_down_scales[:, 4 * q : 4 * q + 4, :])
        load_x(1, 0, C)
        nc.sync.dma_start(out=wd[:], in_=w_kv_down_words.rearrange("g p n t -> p g (n t)").bitcast(I32))
        nc.sync.dma_start(out=wv[:], in_=w_v_up_words[0].rearrange("p n t -> p (n t)").bitcast(I32))
        load_scales(sv, lambda q: w_v_up_scales[0, 4 * q : 4 * q + 4, :].rearrange("r (c n) -> c r n", c=4))
        load_x(2, 0, C)
        nc.sync.dma_start(out=wk[:], in_=w_k_up_words[0].rearrange("p n t -> p (n t)").bitcast(I32))
        load_scales(sk, lambda q: w_k_up_scales[0, 4 * q : 4 * q + 4, :], parts=4)
        load_x(3, 0, C)
        cs = keep.tile([P, 2, DR], BF16)
        nc.gpsimd.dma_start(out=cs[:], in_=freqs_cis.rearrange("(c p) j e -> p c (j e)", p=P))

        cos = keep.tile([P, 2, 2, 32], F32)
        sin = keep.tile([P, 2, 2, 32], F32)

        def make_tables():
            nc.gpsimd.tensor_copy(out=cos[:, :, 0, :], in_=cs[:, :, 0::2])
            nc.gpsimd.tensor_copy(out=cos[:, :, 1, :], in_=cs[:, :, 0::2])
            nc.gpsimd.tensor_scalar(out=sin[:, :, 0, :], in0=cs[:, :, 1::2], scalar1=-1.0, scalar2=None, op0=MULT)
            nc.gpsimd.tensor_copy(out=sin[:, :, 1, :], in_=cs[:, :, 1::2])

        make_tables()

        xb, xq, xqs, acc, kvw, kvq, kvs, ko, vo = ({} for n in range(9))

        def cast(i, a, b, engine="s"):
            if i not in xb:
                x_bf = tok.tile([P, C], BF16, align_bytes=64)
                xb[i] = x_bf
            src = xu[i][:, 512 * a : 512 * b].bitcast(E4M3)
            if engine == "v":
                nc.vector.tensor_copy(out=xb[i][:, 512 * a : 512 * b], in_=src)
            else:
                nc.scalar.copy(out=xb[i][:, 512 * a : 512 * b], in_=src)

        xt = {}

        def turn_x(i, half):
            words = xb[i][:].bitcast(F32)
            t = bank((6, 1)[half] if i == 0 else 0)
            xt[i, half] = t
            for j in range(4):
                g, u = 2 * half + j // 2, j % 2
                nc.tensor.transpose(t[:, P * j : P * (j + 1)], words[:, 256 * g + u : 256 * (g + 1) : 2], ident[:])

        def scale_x(i):
            x_g = tok.tile([P, G, P * 4], BF16, align_bytes=64)
            x_c = tok.tile([P, G * P], I32, align_bytes=64)
            x_s = tok.tile([P, G * P], U8, align_bytes=64)
            xq[i], xqs[i] = x_c, x_s

            def product(g):
                view = xt[i, g // 2][:].bitcast(BF16)[:, 512 * (g % 2) : 512 * (g % 2 + 1)]
                nc.vector.tensor_tensor(
                    out=x_g[:, g, :].rearrange("p (r u e) -> p r u e", u=2, e=2),
                    in0=view.rearrange("p (u r e) -> p r u e", u=2, e=2),
                    in1=xs[:, g, :].unsqueeze(1).to_broadcast([P, P, 4]).rearrange("p r (u e) -> p r u e", e=2),
                    op=MULT,
                )

            def quantise(half):
                nc.vector.quantize_mx(
                    out=x_c[:, 256 * half : 256 * (half + 1)].bitcast(E4M3X4),
                    scales=x_s[:, 256 * half : 256 * (half + 1)],
                    in_=x_g[:, 2 * half : 2 * half + 2, :].rearrange("p g n -> p (g n)"),
                )

            x_ops[i] = (product, quantise)

        x_ops = {}

        def product_x(i, g):
            if i not in x_ops:
                scale_x(i)
            x_ops[i][0](g)

        def quantise_x(i, half):
            x_ops[i][1](half)

        def down(i, half):
            if half == 0:
                a = bank()
                acc[i] = a
            a = acc[i]
            for g in (2 * half, 2 * half + 1):
                nc.tensor.matmul_mx(
                    a[:],
                    lhsT=xq[i][:, P * g : P * (g + 1)].bitcast(E4M3X4),
                    lhsT_scale=xqs[i][:, P * g : P * (g + 1)],
                    rhs=wd[:, g, :].bitcast(E4M3X4),
                    rhs_scale=sd[4 * g : P, :],
                    start=(g == 0),
                    stop=(g == G - 1),
                )

        def round_kv(i, a=0, b=2, engine="s"):
            if i not in kvw:
                kv_b = tok.tile([P, R], BF16, align_bytes=64)
                kvw[i] = kv_b
            copy_out(engine, kvw[i][:, 256 * a : 256 * b], acc[i][:, 256 * a : 256 * b])

        def turn_kv(i):
            t = bank()
            xt[i, "kv"] = t
            words = kvw[i][:].bitcast(F32)
            for u in range(2):
                nc.tensor.transpose(t[:, P * u : P * (u + 1)], words[:, u::2], ident[:])

        def gather_kv(i, engine="v"):
            kv_g = tok.tile([P, R], BF16, align_bytes=64)
            kvw[i] = kv_g
            copy_out(
                engine,
                kv_g[:].bitcast(F32).rearrange("p (r u) -> p r u", u=2),
                xt[i, "kv"][:, 0:256].rearrange("p (u r) -> p r u", u=2),
            )

        def quantise_kv(i):
            kv_c = tok.tile([P, P], I32, align_bytes=64)
            kv_s = tok.tile([P, P], U8, align_bytes=64)
            kvq[i], kvs[i] = kv_c, kv_s
            nc.vector.quantize_mx(out=kv_c[:].bitcast(E4M3X4), scales=kv_s[:], in_=kvw[i][:])

        def up(i, out, codes, scales):
            nc.tensor.matmul_mx(
                out,
                lhsT=kvq[i][:].bitcast(E4M3X4),
                lhsT_scale=kvs[i][:],
                rhs=codes.bitcast(E4M3X4),
                rhs_scale=scales,
                start=True,
                stop=True,
            )

        def copy_out(engine, out, in_):
            if engine == "v":
                nc.vector.tensor_copy(out=out, in_=in_)
            else:
                nc.scalar.copy(out=out, in_=in_)

        banks = {}

        def begin_out(i):
            k_sb = tok.tile([P, H, DQ], F32, align_bytes=64)
            v_sb = tok.tile([P, H * DV], F32, align_bytes=64)
            ko[i], vo[i] = k_sb, v_sb

        def mm_v(i, c):
            b = bank()
            banks["v", i, c] = b
            up(i, b[:], wv[:, 512 * c : 512 * (c + 1)], sv[4 * c : P, :])

        def ev_v(i, c, engine="s"):
            copy_out(engine, vo[i][:, 512 * c : 512 * (c + 1)], banks["v", i, c][:])

        def store_v(i, c0, c1):
            nc.sync.dma_start(out=v_rows[i // 2][:, i % 2, 512 * c0 : 512 * c1], in_=vo[i][:, 512 * c0 : 512 * c1])

        def mm_n(i, c):
            b = bank()
            banks["n", i, c] = b
            for j in range(4):
                h = 4 * c + j
                up(i, b[:, DN * j : DN * (j + 1)], wk[:, DQ * h : DQ * h + DN], sk[:, DQ * h : DQ * h + DN])

        def ev_n(i, c, engine="s"):
            copy_out(engine, ko[i][:, 4 * c : 4 * c + 4, 0:DN], banks["n", i, c][:].rearrange("p (h d) -> p h d", d=DN))

        def mm_r(i, half):
            b = bank()
            banks["r", i, half] = b
            for j in range(8):
                h = 8 * half + j
                up(
                    i,
                    b[:, DR * j : DR * (j + 1)],
                    wk[:, DQ * h + DN : DQ * (h + 1)],
                    sk[:, DQ * h + DN : DQ * (h + 1)],
                )

        def ev_r(i, half, add_engine="v"):
            r = banks["r", i, half][:].rearrange("p (h a j) -> p h a j", a=2, j=32)
            rc = rot.tile([P, 8, 2, 32], F32)
            rs = rot.tile([P, 8, 2, 32], F32)
            par = i % 2
            cb = cos[:, par].unsqueeze(1).to_broadcast([P, 8, 2, 32])
            sb = sin[:, par].unsqueeze(1).to_broadcast([P, 8, 2, 32])
            nc.vector.tensor_tensor(out=rc[:], in0=r, in1=cb, op=MULT)
            nc.vector.tensor_tensor(out=rs[:], in0=r[:, :, ::-1, :], in1=sb, op=MULT)
            eng = nc.gpsimd if add_engine == "g" else nc.vector
            eng.tensor_tensor(
                out=ko[i][:, 8 * half : 8 * half + 8, DN:DQ],
                in0=rc[:].rearrange("p h a j -> p h (a j)"),
                in1=rs[:].rearrange("p h a j -> p h (a j)"),
                op=ADD,
            )

        def store_k(i, h0, h1):
            hs = slice(8 * h0, 8 * h1)
            nc.sync.dma_start(out=k_rows[i // 2][:, i % 2, hs, :], in_=ko[i][:, hs, :])

        cast(0, 0, 1, "v")
        cast(0, 1, 2, "v")
        turn_x(0, 0)
        cast(0, 3, 4, "v")
        cast(0, 2, 3)
        product_x(0, 0)
        product_x(0, 1)
        turn_x(0, 1)
        cast(1, 0, 2)
        product_x(0, 2)
        cast(1, 2, 4)
        quantise_x(0, 0)
        turn_x(1, 0)
        product_x(0, 3)
        product_x(1, 1)
        down(0, 0)
        quantise_x(0, 1)
        turn_x(1, 1)
        down(0, 1)
        round_kv(0, 0, 1)
        product_x(1, 0)
        product_x(1, 2)
        round_kv(0, 1, 2)
        quantise_x(1, 0)
        cast(2, 2, 4)
        product_x(1, 3)
        quantise_x(1, 1)
        cast(2, 0, 2, "v")
        down(1, 0)
        turn_kv(0)
        down(1, 1)
        gather_kv(0)
        turn_x(2, 0)
        round_kv(1, 0, 2)
        turn_x(2, 1)
        quantise_kv(0)
        turn_kv(1)
        product_x(2, 0)
        product_x(2, 1)
        product_x(2, 3)
        mm_v(0, 0)
        gather_kv(1, "s")
        mm_v(0, 1)
        begin_out(0)
        ev_v(0, 0)
        store_v(0, 0, 1)
        mm_v(0, 2)
        mm_v(0, 3)
        quantise_kv(1)
        mm_v(1, 0)
        mm_v(1, 1)
        mm_v(1, 3)
        mm_v(1, 2)
        quantise_x(2, 0)
        ev_v(0, 1)
        store_v(0, 1, 2)
        ev_v(0, 3)
        ev_v(0, 2, "v")
        store_v(0, 2, 4)
        down(2, 0)
        product_x(2, 2)
        begin_out(1)
        ev_v(1, 1)
        mm_r(0, 1)
        cast(3, 0, 2, "v")
        mm_n(0, 3)
        ev_v(1, 2)
        ev_v(1, 0)
        ev_v(1, 3, "v")
        store_v(1, 0, 4)
        quantise_x(2, 1)
        ev_r(0, 1, "g")
        mm_r(1, 0)
        mm_n(0, 2)
        cast(3, 2, 4)
        mm_n(1, 0)
        mm_r(1, 1)
        ev_n(0, 3)
        ev_n(1, 0)
        down(2, 1)
        mm_n(1, 2)
        mm_n(1, 1)
        mm_r(0, 0)
        mm_n(1, 3)
        round_kv(2, 0, 2)
        ev_n(1, 1)
        ev_n(0, 2, "v")
        store_k(0, 1, 2)
        turn_kv(2)
        ev_r(1, 0, "g")
        store_k(1, 0, 1)
        gather_kv(2, "s")
        ev_r(1, 1, "g")
        ev_r(0, 0, "g")
        turn_x(3, 0)
        ev_n(1, 3)
        turn_x(3, 1)
        mm_n(0, 1)
        ev_n(1, 2)
        store_k(1, 1, 2)
        mm_n(0, 0)
        quantise_kv(2)
        ev_n(0, 1)
        product_x(3, 0)
        product_x(3, 1)
        product_x(3, 3)
        mm_v(2, 3)
        mm_v(2, 2)
        mm_r(2, 0)
        ev_n(0, 0)
        store_k(0, 0, 1)
        mm_v(2, 1)
        mm_v(2, 0)
        begin_out(2)
        ev_v(2, 3)
        product_x(3, 2)
        quantise_x(3, 0)
        down(3, 0)
        quantise_x(3, 1)
        down(3, 1)
        mm_n(2, 0)
        mm_n(2, 1)
        mm_n(2, 3)
        ev_v(2, 2)
        ev_v(2, 1)
        ev_v(2, 0, "v")
        store_v(2, 0, 4)
        ev_r(2, 0)
        round_kv(3, 0, 2)
        turn_kv(3)
        gather_kv(3)
        quantise_kv(3)
        mm_r(2, 1)
        ev_n(2, 0)
        ev_n(2, 1)
        store_k(2, 0, 1)
        mm_v(3, 3)
        mm_v(3, 2)
        mm_v(3, 0)
        mm_v(3, 1)
        begin_out(3)
        ev_v(3, 2)
        ev_n(2, 3, "v")
        mm_r(3, 0)
        mm_n(3, 0)
        mm_n(2, 2)
        mm_r(3, 1)
        ev_v(3, 0)
        ev_v(3, 3, "v")
        store_v(3, 2, 4)
        mm_n(3, 1)
        ev_v(3, 1)
        store_v(3, 0, 2)
        ev_n(3, 0)
        ev_n(2, 2)
        ev_n(3, 1)
        mm_n(3, 2)
        mm_n(3, 3)
        ev_r(2, 1, "g")
        store_k(2, 1, 2)
        ev_r(3, 0, "g")
        store_k(3, 0, 1)
        ev_r(3, 1)
        ev_n(3, 2)
        ev_n(3, 3)
        store_k(3, 1, 2)
